import numpy as np
import ml_dtypes


def mxq(x, axis, fmt="e4m3"):
    dtype, down = {"e4m3": (ml_dtypes.float8_e4m3fn, 7), "e5m2": (ml_dtypes.float8_e5m2, 14)}[fmt]
    v = np.moveaxis(np.asarray(x, np.float32).astype(ml_dtypes.bfloat16).astype(np.float64), axis, -1)
    blocks = v.reshape(v.shape[:-1] + (-1, 32))
    amax = np.abs(blocks).max(-1, keepdims=True)
    byte = np.maximum(np.where(amax > 0, np.frexp(amax)[1] - 1 + 127, 0) - down, 1)
    scale = np.exp2(byte - 127.0)
    codes = (blocks / scale).astype(np.float32).astype(dtype).astype(np.float64)
    return np.moveaxis((codes * scale).reshape(v.shape), -1, axis)


WIDE = False


def mx_kscale(k):
    if not WIDE:
        return np.ones(k)
    levels = np.array([10, -10, 5, -5, 0])
    a = np.random.permutation(np.resize(levels, k // 512 * 4)).reshape(k // 512, 4)
    idx = np.arange(k)
    return np.exp2(a[idx // 512, idx % 128 // 32])


BF16 = ml_dtypes.bfloat16


def bf(x):
    return np.asarray(x, np.float32).astype(BF16)


def f64(x):
    return np.asarray(x).astype(np.float64)


H, I, B = 1024, 1024, 512


def sigmoid(v):
    return 1.0 / (1.0 + np.exp(-v))


def log_sigmoid(v):
    return np.minimum(v, 0.0) - np.log(1.0 + np.exp(-np.abs(v)))


def setup_inputs():
    s, t = mx_kscale(I), mx_kscale(H)

    def w():
        return bf(np.random.standard_normal((H, I)) * 0.7 / np.sqrt(I) / s)

    def r():
        return bf(np.random.standard_normal((H, H)) * 0.7 / np.sqrt(H) / t)

    def b():
        return bf(np.random.standard_normal(H) * 0.3)

    return {"x": bf(np.random.standard_normal((I, B)) * s[:, None]),
            "h_prev": bf(np.random.standard_normal((H, B)) * t[:, None]),
            "c_prev": bf(np.random.standard_normal((H, B))),
            "n_prev": bf(np.random.uniform(size=(H, B))),
            "m_prev": bf(np.random.standard_normal((H, B))),
            "w_input": w(), "w_forget": w(), "w_output": w(), "w_z": w(),
            "r_input": r(), "r_forget": r(), "r_output": r(), "r_z": r(),
            "b_input": b(), "b_forget": b(), "b_output": b(), "b_z": b()}


def reference(x, h_prev, c_prev, n_prev, m_prev,
              w_input, w_forget, w_output, w_z,
              r_input, r_forget, r_output, r_z,
              b_input, b_forget, b_output, b_z):
    xq = mxq(f64(x), 0, "e4m3")
    hq = mxq(f64(h_prev), 0, "e4m3")
    input_wave = (mxq(f64(w_input), 1, "e4m3") @ xq) + (mxq(f64(r_input), 1, "e4m3") @ hq) + f64(b_input)[:, None]
    forget_wave = (mxq(f64(w_forget), 1, "e4m3") @ xq) + (mxq(f64(r_forget), 1, "e4m3") @ hq) + f64(b_forget)[:, None]
    output_wave = (mxq(f64(w_output), 1, "e4m3") @ xq) + (mxq(f64(r_output), 1, "e4m3") @ hq) + f64(b_output)[:, None]
    z_wave = (mxq(f64(w_z), 1, "e4m3") @ xq) + (mxq(f64(r_z), 1, "e4m3") @ hq) + f64(b_z)[:, None]

    log_i = input_wave
    log_f = log_sigmoid(forget_wave)
    m_t = np.maximum(log_f + f64(m_prev), log_i)
    input_prime = np.exp(log_i - m_t)
    forget_prime = np.exp(log_f + f64(m_prev) - m_t)

    c_t = forget_prime * f64(c_prev) + input_prime * np.tanh(z_wave)
    n_t = forget_prime * f64(n_prev) + forget_prime
    h_wave = c_t / n_t
    h_t = sigmoid(output_wave) * np.tanh(h_wave)
    return (h_t, c_t, n_t, m_t)

@@ -1,0 +1,269 @@
+from contextlib import ExitStack
+
+import concourse.mybir as mybir
+from concourse.masks import make_identity
+
+F32 = mybir.dt.float32
+BF16 = mybir.dt.bfloat16
+U32 = mybir.dt.uint32
+U8 = mybir.dt.uint8
+FP8X4 = mybir.dt.float8_e4m3fn_x4
+ACT = mybir.ActivationFunctionType
+ALU = mybir.AluOpType
+
+P = 128
+FEATURES = 1024
+BATCH = 512
+TILES = FEATURES // P
+PACK = 4
+K_PASS = P * PACK
+PASSES = FEATURES // K_PASS
+GATES = 4
+UNITS = GATES * TILES
+FORGET, INPUT, CELL, OUTPUT = range(GATES)
+WORDS = FEATURES // 2
+
+FLOPS = 2 * 2 * GATES * FEATURES * FEATURES * BATCH
+
+AT_FORGET = FORGET * TILES + 1
+AT_LOGS = AT_FORGET + TILES - 1
+AT_INPUT = INPUT * TILES + 1
+AT_CELL = CELL * TILES + 1
+AT_OUTPUT = OUTPUT * TILES + 1
+AT_EXP = AT_INPUT + 3
+AT_SPAN = AT_INPUT + 1
+AT_NORM = AT_OUTPUT - 3
+RAW_AHEAD = 10
+
+
+def tile_slstmcell_pa_kernel(
+    tc, x, h_prev, c_prev, n_prev, m_prev,
+    w_input, w_forget, w_output, w_z, r_input, r_forget, r_output, r_z,
+    b_input, b_forget, b_output, b_z,
+    out_0, out_1, out_2, out_3,
+):
+    nc = tc.nc
+    w_of = (w_forget, w_input, w_z, w_output)
+    r_of = (r_forget, r_input, r_z, r_output)
+    b_of = (b_forget, b_input, b_z, b_output)
+
+    def by_tile(a):
+        return a.rearrange("(p t) c -> p t c", t=TILES)
+
+    h_out, c_out, n_out, m_out = by_tile(out_0), by_tile(out_1), by_tile(out_2), by_tile(out_3)
+
+    with ExitStack() as ctx:
+        ctx.enter_context(tc.manual_schedule())
+        consts = ctx.enter_context(tc.tile_pool(name="consts", bufs=1))
+        raw_pool = ctx.enter_context(tc.tile_pool(name="raw", bufs=RAW_AHEAD))
+        grouped_pool = ctx.enter_context(tc.tile_pool(name="grouped", bufs=3))
+        codes_pool = ctx.enter_context(tc.tile_pool(name="codes", bufs=3))
+        state = ctx.enter_context(tc.tile_pool(name="state", bufs=TILES))
+        temps = ctx.enter_context(tc.tile_pool(name="temps", bufs=3))
+        results = ctx.enter_context(tc.tile_pool(name="results", bufs=3))
+        turned_pool = ctx.enter_context(tc.psum_pool(name="turned", bufs=4))
+        wave_pool = ctx.enter_context(tc.psum_pool(name="waves", bufs=4))
+
+        identity = consts.tile([P, P], F32, name="identity")
+        make_identity(nc, identity[:])
+        one = consts.tile([P, 1], F32, name="one")
+        nc.vector.memset(one[:], 1.0)
+        bias_bf = consts.tile([P, GATES, 2 * TILES], BF16, name="bias_bf")
+        for gate in range(GATES):
+            nc.scalar.dma_start(out=bias_bf[:, gate, 0:TILES], in_=b_of[gate].rearrange("(p t) -> p t", t=TILES))
+        bias = consts.tile([P, GATES, TILES], F32, name="bias")
+        nc.vector.tensor_copy(out=bias[:], in_=bias_bf[:, :, 0:TILES])
+        minus_bias_f = consts.tile([P, TILES], F32, name="minus_bias_f")
+        nc.vector.tensor_scalar(out=minus_bias_f[:], in0=bias[:, FORGET, :], scalar1=-1.0, scalar2=None, op0=ALU.mult)
+        half_bias_o = consts.tile([P, TILES], F32, name="half_bias_o")
+        nc.vector.tensor_scalar(out=half_bias_o[:], in0=bias[:, OUTPUT, :], scalar1=0.5, scalar2=None, op0=ALU.mult)
+
+        moving_codes = consts.tile([P, 2 * PASSES, BATCH], U32, name="moving_codes", align_bytes=64)
+        moving_scales = consts.tile([P, 2 * PASSES, BATCH], U8, name="moving_scales", align_bytes=64)
+        m_old = consts.tile([P, TILES, BATCH], BF16, name="m_old")
+        n_old = consts.tile([P, TILES, BATCH], BF16, name="n_old")
+        c_old = consts.tile([P, TILES, BATCH], BF16, name="c_old")
+
+        moving_raw = []
+        for source in (x, h_prev):
+            halves = source.rearrange("(g u q e) b -> q g u (e b)", g=PASSES, u=2, e=2)
+            for g in range(PASSES):
+                raw = raw_pool.tile([P, PACK, BATCH], BF16, tag="raw", name="moving_raw%d" % len(moving_raw))
+                nc.sync.dma_start(out=raw[:].rearrange("q (u e) b -> q u (e b)", e=2), in_=halves[:, g])
+                moving_raw.append(raw)
+
+        raw_of = {}
+
+        def load_pair(pair):
+            gate, first = divmod(2 * pair, TILES)
+            for m, matrix in enumerate((w_of[gate], r_of[gate])):
+                raw = raw_pool.tile([P, 2, FEATURES], BF16, tag="raw", name="raw%d_%d" % (pair, m))
+                nc.sync.dma_start(out=raw[:], in_=by_tile(matrix)[:, first : first + 2, :])
+                raw_of[(pair, m)] = raw
+            if gate == FORGET:
+                nc.sync.dma_start(out=m_old[:, first : first + 2, :], in_=by_tile(m_prev)[:, first : first + 2, :])
+            if pair == TILES // 2 - 1:
+                nc.sync.dma_start(out=n_old[:], in_=by_tile(n_prev))
+            if pair == TILES // 2 + 1:
+                nc.sync.dma_start(out=c_old[:], in_=by_tile(c_prev))
+
+        for pair in range(3):
+            load_pair(pair)
+
+        for j in range(2 * PASSES):
+            grouped = grouped_pool.tile([P, BATCH, PACK], BF16, tag="grouped", name="moving_grouped%d" % j, align_bytes=64)
+            nc.vector.tensor_copy(
+                out=grouped[:].rearrange("p (c i) t -> p c t i", i=4),
+                in_=moving_raw[j][:].rearrange("p t (c i) -> p c t i", i=4),
+            )
+            nc.vector.quantize_mx(
+                out=moving_codes[:, j, :].bitcast(FP8X4),
+                scales=moving_scales[:, j, :],
+                in_=grouped[:].rearrange("p b t -> p (b t)"),
+            )
+
+        banks_of, grouped_of, codes_of, scales_of, wave_of = {}, {}, {}, {}, {}
+
+        def turn(u):
+            for m in range(2):
+                words = raw_of[(u // 2, m)][:, u % 2, :].bitcast(F32)
+                bank = turned_pool.tile([P, 2 * PASSES, P], F32, tag="turned", name="turned%d_%d" % (u, m))
+                for c in range(2 * PASSES):
+                    nc.tensor.transpose(bank[:, c, :], words[:, c * P : (c + 1) * P], identity[:])
+                banks_of[(u, m)] = bank
+
+        def evacuate(u, m, engine_copy):
+            if m == 0:
+                grouped_of[u] = grouped_pool.tile([P, 2 * FEATURES], BF16, tag="grouped", name="grouped%d" % u, align_bytes=64)
+            pairs = grouped_of[u][:].bitcast(F32)[:, m * WORDS : (m + 1) * WORDS]
+            engine_copy(
+                out=pairs.rearrange("p (g h u) -> p g h u", g=PASSES, u=2),
+                in_=banks_of[(u, m)][:].rearrange("p (g u) h -> p g h u", u=2),
+            )
+
+        def quantise(u):
+            codes_of[u] = codes_pool.tile([P, 2 * PASSES * P], U32, tag="codes", name="codes%d" % u, align_bytes=64)
+            scales_of[u] = codes_pool.tile([P, 2 * PASSES * P], U8, tag="scales", name="scales%d" % u, align_bytes=64)
+            nc.vector.quantize_mx(out=codes_of[u][:].bitcast(FP8X4), scales=scales_of[u][:], in_=grouped_of[u][:])
+
+        def multiply(u):
+            wave_of[u] = wave_pool.tile([P, BATCH], F32, tag="wave", name="wave%d" % u)
+            for j in range(2 * PASSES):
+                cols = slice(j * P, (j + 1) * P)
+                nc.tensor.matmul_mx(
+                    out=wave_of[u][:],
+                    lhsT=codes_of[u][:, cols].bitcast(FP8X4),
+                    lhsT_scale=scales_of[u][:, cols],
+                    rhs=moving_codes[:, j, :].bitcast(FP8X4),
+                    rhs_scale=moving_scales[:, j, :],
+                    start=(j == 0),
+                    stop=(j == 2 * PASSES - 1),
+                )
+
+        m_plus_b, soft, log_fm, log_n1, gap, span, old_part, shrink, z_part, h_wave, o_part = ({} for k in range(11))
+
+        def column(table, t):
+            return table[:, t : t + 1]
+
+        def in_tiles(t):
+            return 0 <= t < TILES
+
+        for s in range(-3, UNITS + 2):
+            if s % 2 == 0 and 3 <= (s + 8) // 2 < UNITS // 2:
+                load_pair((s + 8) // 2)
+            if 0 <= s < UNITS:
+                multiply(s)
+            if 0 <= s + 3 < UNITS:
+                turn(s + 3)
+
+            t = s - AT_FORGET
+            if in_tiles(t):
+                soft[t] = state.tile([P, BATCH], F32, tag="soft_gap", name="soft%d" % t)
+                nc.scalar.activation(out=soft[t][:], in_=wave_of[t][:], func=ACT.Abs, bias=column(bias[:, FORGET, :], t), scale=1.0)
+            nxt = s + 1
+            if 0 <= s + 2 < UNITS:
+                evacuate(s + 2, 0, nc.scalar.copy)
+                if (s + 2) // TILES in (FORGET, OUTPUT):
+                    evacuate(s + 2, 1, nc.vector.tensor_copy)
+                else:
+                    evacuate(s + 2, 1, nc.scalar.copy)
+            if in_tiles(t):
+                nc.scalar.activation(out=soft[t][:], in_=soft[t][:], func=ACT.Exp, scale=-1.0)
+                log_fm[t] = state.tile([P, BATCH], F32, tag="log_fm_h", name="log_fm%d" % t)
+                nc.vector.scalar_tensor_tensor(
+                    out=log_fm[t][:], in0=wave_of[t][:], scalar=column(minus_bias_f, t), in1=m_plus_b[t][:], op0=ALU.min, op1=ALU.add
+                )
+            t = s - AT_INPUT
+            if in_tiles(t):
+                nc.vector.tensor_tensor(out=log_fm[t][:], in0=log_fm[t][:], in1=soft[t][:], op=ALU.subtract)
+            if 0 <= nxt < UNITS:
+                quantise(nxt)
+            if in_tiles(t):
+                wave = wave_of[INPUT * TILES + t]
+                gap[t] = state.tile([P, BATCH], F32, tag="soft_gap", name="gap%d" % t)
+                nc.vector.scalar_tensor_tensor(
+                    out=gap[t][:], in0=wave[:], scalar=column(bias[:, INPUT, :], t), in1=log_fm[t][:], op0=ALU.add, op1=ALU.subtract
+                )
+                m_new = results.tile([P, BATCH], F32, tag="m_new", name="m_new%d" % t)
+                nc.vector.scalar_tensor_tensor(
+                    out=m_new[:], in0=wave[:], scalar=column(bias[:, INPUT, :], t), in1=log_fm[t][:], op0=ALU.add, op1=ALU.max
+                )
+                nc.sync.dma_start(out=m_out[:, t, :], in_=m_new[:])
+            t = s - AT_CELL
+            if in_tiles(t):
+                z_part[t] = temps.tile([P, BATCH], F32, tag="z_part", name="z_part%d" % t)
+                nc.scalar.activation(out=z_part[t][:], in_=wave_of[CELL * TILES + t][:], func=ACT.Tanh, bias=column(bias[:, CELL, :], t), scale=1.0)
+            t = s - AT_OUTPUT
+            if in_tiles(t):
+                o_part[t] = results.tile([P, BATCH], F32, tag="h_new", name="o_part%d" % t)
+                nc.scalar.activation(out=o_part[t][:], in_=wave_of[OUTPUT * TILES + t][:], func=ACT.Tanh, bias=column(half_bias_o, t), scale=0.5)
+            j = s - AT_LOGS
+            if 0 <= j < TILES // 2:
+                for t in (2 * j, 2 * j + 1):
+                    nc.scalar.activation(out=soft[t][:], in_=soft[t][:], func=ACT.Ln, bias=one[:], scale=1.0)
+                    log_n1[t] = state.tile([P, BATCH], F32, tag="log_n1", name="log_n1_%d" % t)
+                    nc.scalar.activation(out=log_n1[t][:], in_=n_old[:, t, :], func=ACT.Ln, bias=one[:], scale=1.0)
+            t = s - AT_SPAN
+            if in_tiles(t):
+                span[t] = state.tile([P, BATCH], F32, tag="span", name="span%d" % t)
+                nc.vector.scalar_tensor_tensor(out=span[t][:], in0=gap[t][:], scalar=0.0, in1=log_n1[t][:], op0=ALU.max, op1=ALU.subtract)
+            t = s - AT_CELL - 1
+            if in_tiles(t):
+                nc.vector.scalar_tensor_tensor(out=z_part[t][:], in0=gap[t][:], scalar=1.0, in1=z_part[t][:], op0=ALU.min, op1=ALU.mult)
+            t = s - AT_EXP - 1
+            if in_tiles(t):
+                old_part[t] = state.tile([P, BATCH], F32, tag="old_part", name="old_part%d" % t)
+                nc.vector.scalar_tensor_tensor(out=old_part[t][:], in0=shrink[t][:], scalar=1.0, in1=c_old[:, t, :], op0=ALU.min, op1=ALU.mult)
+            t = s - AT_CELL - 1
+            if in_tiles(t):
+                nc.vector.tensor_tensor(out=old_part[t][:], in0=old_part[t][:], in1=z_part[t][:], op=ALU.add)
+                nc.sync.dma_start(out=c_out[:, t, :], in_=old_part[t][:])
+            t = s - AT_NORM - 3
+            if in_tiles(t):
+                nc.vector.tensor_scalar(out=h_wave[t][:], in0=h_wave[t][:], scalar1=0.5, scalar2=None, op0=ALU.mult)
+            t = s - AT_NORM - 1
+            if in_tiles(t):
+                h_wave[t] = state.tile([P, BATCH], F32, tag="log_fm_h", name="h_wave%d" % t)
+                nc.vector.tensor_tensor(out=h_wave[t][:], in0=old_part[t][:], in1=span[t][:], op=ALU.mult)
+            t = s
+            if in_tiles(t):
+                m_plus_b[t] = temps.tile([P, BATCH], F32, tag="m_plus_b", name="m_plus_b%d" % t)
+                nc.vector.tensor_scalar(out=m_plus_b[t][:], in0=m_old[:, t, :], scalar1=column(bias[:, FORGET, :], t), scalar2=None, op0=ALU.add)
+            t = s - AT_OUTPUT
+            if in_tiles(t):
+                nc.vector.scalar_tensor_tensor(out=o_part[t][:], in0=o_part[t][:], scalar=1.0, in1=h_wave[t][:], op0=ALU.add, op1=ALU.mult)
+                nc.sync.dma_start(out=h_out[:, t, :], in_=o_part[t][:])
+            t = s - AT_EXP
+            if in_tiles(t):
+                shrink[t] = temps.tile([P, BATCH], F32, tag="shrink", name="shrink%d" % t)
+                nc.scalar.activation(out=shrink[t][:], in_=gap[t][:], func=ACT.Exp, scale=-1.0)
+                nc.scalar.activation(out=gap[t][:], in_=gap[t][:], func=ACT.Exp, scale=1.0)
+            t = s - AT_NORM
+            if in_tiles(t):
+                n_new = results.tile([P, BATCH], F32, tag="n_new", name="n_new%d" % t)
+                nc.scalar.activation(out=n_new[:], in_=span[t][:], func=ACT.Exp, scale=-1.0)
+                nc.sync.dma_start(out=n_out[:, t, :], in_=n_new[:])
+                nc.scalar.activation(out=span[t][:], in_=span[t][:], func=ACT.Exp, scale=1.0)
+            t = s - AT_NORM - 2
+            if in_tiles(t):
+                nc.scalar.activation(out=h_wave[t][:], in_=h_wave[t][:], func=ACT.Tanh, scale=1.0)

@@ -22,7 +22,6 @@ GATES = 4
 UNITS = GATES * TILES
 FORGET, INPUT, CELL, OUTPUT = range(GATES)
 WORDS = FEATURES // 2
-
 FLOPS = 2 * 2 * GATES * FEATURES * FEATURES * BATCH
 
 AT_FORGET = FORGET * TILES + 1
@@ -32,8 +31,9 @@ AT_CELL = CELL * TILES + 1
 AT_OUTPUT = OUTPUT * TILES + 1
 AT_EXP = AT_INPUT + 3
 AT_SPAN = AT_INPUT + 1
-AT_NORM = AT_OUTPUT - 3
+AT_NORM = AT_OUTPUT - 4
 RAW_AHEAD = 10
+VECTOR_COLUMNS = 336
 
 
 def tile_slstmcell_pa_kernel(
@@ -58,25 +58,17 @@ def tile_slstmcell_pa_kernel(
         raw_pool = ctx.enter_context(tc.tile_pool(name="raw", bufs=RAW_AHEAD))
         grouped_pool = ctx.enter_context(tc.tile_pool(name="grouped", bufs=3))
         codes_pool = ctx.enter_context(tc.tile_pool(name="codes", bufs=3))
-        state = ctx.enter_context(tc.tile_pool(name="state", bufs=TILES))
-        temps = ctx.enter_context(tc.tile_pool(name="temps", bufs=3))
-        results = ctx.enter_context(tc.tile_pool(name="results", bufs=3))
+        state = ctx.enter_context(tc.tile_pool(name="state", bufs=TILES // 2))
+        temps = ctx.enter_context(tc.tile_pool(name="temps", bufs=2))
+        results = ctx.enter_context(tc.tile_pool(name="results", bufs=2))
         turned_pool = ctx.enter_context(tc.psum_pool(name="turned", bufs=4))
         wave_pool = ctx.enter_context(tc.psum_pool(name="waves", bufs=4))
 
         identity = consts.tile([P, P], F32, name="identity")
         make_identity(nc, identity[:])
-        one = consts.tile([P, 1], F32, name="one")
-        nc.vector.memset(one[:], 1.0)
         bias_bf = consts.tile([P, GATES, 2 * TILES], BF16, name="bias_bf")
         for gate in range(GATES):
             nc.scalar.dma_start(out=bias_bf[:, gate, 0:TILES], in_=b_of[gate].rearrange("(p t) -> p t", t=TILES))
-        bias = consts.tile([P, GATES, TILES], F32, name="bias")
-        nc.vector.tensor_copy(out=bias[:], in_=bias_bf[:, :, 0:TILES])
-        minus_bias_f = consts.tile([P, TILES], F32, name="minus_bias_f")
-        nc.vector.tensor_scalar(out=minus_bias_f[:], in0=bias[:, FORGET, :], scalar1=-1.0, scalar2=None, op0=ALU.mult)
-        half_bias_o = consts.tile([P, TILES], F32, name="half_bias_o")
-        nc.vector.tensor_scalar(out=half_bias_o[:], in0=bias[:, OUTPUT, :], scalar1=0.5, scalar2=None, op0=ALU.mult)
 
         moving_codes = consts.tile([P, 2 * PASSES, BATCH], U32, name="moving_codes", align_bytes=64)
         moving_scales = consts.tile([P, 2 * PASSES, BATCH], U8, name="moving_scales", align_bytes=64)
@@ -107,20 +99,29 @@ def tile_slstmcell_pa_kernel(
             if pair == TILES // 2 + 1:
                 nc.sync.dma_start(out=c_old[:], in_=by_tile(c_prev))
 
-        for pair in range(3):
+        for pair in range((RAW_AHEAD - 4) // 2):
             load_pair(pair)
 
         for j in range(2 * PASSES):
             grouped = grouped_pool.tile([P, BATCH, PACK], BF16, tag="grouped", name="moving_grouped%d" % j, align_bytes=64)
-            nc.vector.tensor_copy(
-                out=grouped[:].rearrange("p (c i) t -> p c t i", i=4),
-                in_=moving_raw[j][:].rearrange("p t (c i) -> p c t i", i=4),
-            )
-            nc.vector.quantize_mx(
-                out=moving_codes[:, j, :].bitcast(FP8X4),
-                scales=moving_scales[:, j, :],
-                in_=grouped[:].rearrange("p b t -> p (b t)"),
-            )
+            for engine_copy, cols in ((nc.vector.tensor_copy, slice(0, VECTOR_COLUMNS)), (nc.scalar.copy, slice(VECTOR_COLUMNS, BATCH))):
+                engine_copy(
+                    out=grouped[:, cols, :].rearrange("p (c i) t -> p c t i", i=4),
+                    in_=moving_raw[j][:, :, cols].rearrange("p t (c i) -> p c t i", i=4),
+                )
+            if j > 0:
+                nc.vector.quantize_mx(out=moving_codes[:, j - 1, :].bitcast(FP8X4), scales=moving_scales[:, j - 1, :], in_=previous[:].rearrange("p b t -> p (b t)"))
+            previous = grouped
+        nc.vector.quantize_mx(out=moving_codes[:, 3, :].bitcast(FP8X4), scales=moving_scales[:, 3, :], in_=previous[:].rearrange("p b t -> p (b t)"))
+
+        one = consts.tile([P, 1], F32, name="one")
+        nc.vector.memset(one[:], 1.0)
+        bias = consts.tile([P, GATES, TILES], F32, name="bias")
+        nc.vector.tensor_copy(out=bias[:], in_=bias_bf[:, :, 0:TILES])
+        minus_bias_f = consts.tile([P, TILES], F32, name="minus_bias_f")
+        nc.vector.tensor_scalar(out=minus_bias_f[:], in0=bias[:, FORGET, :], scalar1=-1.0, scalar2=None, op0=ALU.mult)
+        half_bias_o = consts.tile([P, TILES], F32, name="half_bias_o")
+        nc.vector.tensor_scalar(out=half_bias_o[:], in0=bias[:, OUTPUT, :], scalar1=0.5, scalar2=None, op0=ALU.mult)
 
         banks_of, grouped_of, codes_of, scales_of, wave_of = {}, {}, {}, {}, {}
 
@@ -133,7 +134,7 @@ def tile_slstmcell_pa_kernel(
                 banks_of[(u, m)] = bank
 
         def evacuate(u, m, engine_copy):
-            if m == 0:
+            if u not in grouped_of:
                 grouped_of[u] = grouped_pool.tile([P, 2 * FEATURES], BF16, tag="grouped", name="grouped%d" % u, align_bytes=64)
             pairs = grouped_of[u][:].bitcast(F32)[:, m * WORDS : (m + 1) * WORDS]
             engine_copy(
@@ -151,119 +152,157 @@ def tile_slstmcell_pa_kernel(
             for j in range(2 * PASSES):
                 cols = slice(j * P, (j + 1) * P)
                 nc.tensor.matmul_mx(
-                    out=wave_of[u][:],
-                    lhsT=codes_of[u][:, cols].bitcast(FP8X4),
-                    lhsT_scale=scales_of[u][:, cols],
-                    rhs=moving_codes[:, j, :].bitcast(FP8X4),
-                    rhs_scale=moving_scales[:, j, :],
-                    start=(j == 0),
-                    stop=(j == 2 * PASSES - 1),
+                    out=wave_of[u][:], lhsT=codes_of[u][:, cols].bitcast(FP8X4), lhsT_scale=scales_of[u][:, cols],
+                    rhs=moving_codes[:, j, :].bitcast(FP8X4), rhs_scale=moving_scales[:, j, :],
+                    start=(j == 0), stop=(j == 2 * PASSES - 1),
                 )
 
-        m_plus_b, soft, log_fm, log_n1, gap, span, old_part, shrink, z_part, h_wave, o_part = ({} for k in range(11))
+        m_plus_b, soft, log_fm, log_n1, gap, span, old_part, shrink, z_part, h_wave, o_part, m_new = ({} for k in range(12))
+        PAIRS = TILES // 2
 
         def column(table, t):
             return table[:, t : t + 1]
 
-        def in_tiles(t):
-            return 0 <= t < TILES
+        def pair_tile(pool, tag, j):
+            return pool.tile([P, 2, BATCH], F32, tag=tag, name="%s%d" % (tag, j))
 
-        for s in range(-3, UNITS + 2):
-            if s % 2 == 0 and 3 <= (s + 8) // 2 < UNITS // 2:
-                load_pair((s + 8) // 2)
+        def s_magnitude(t):
+            if t % 2 == 0:
+                soft[t // 2] = pair_tile(state, "soft_gap", t // 2)
+            nc.scalar.activation(out=soft[t // 2][:, t % 2, :], in_=wave_of[t][:], func=ACT.Abs, bias=column(bias[:, FORGET, :], t), scale=1.0)
+
+        def v_floor(t):
+            if t % 2 == 0:
+                log_fm[t // 2] = pair_tile(state, "log_fm_h", t // 2)
+            nc.vector.scalar_tensor_tensor(out=log_fm[t // 2][:, t % 2, :], in0=wave_of[t][:], scalar=column(minus_bias_f, t), in1=m_plus_b[t // 2][:, t % 2, :], op0=ALU.min, op1=ALU.add)
+
+        def v_input(t):
+            wave = wave_of[INPUT * TILES + t]
+            if t % 2 == 0:
+                gap[t // 2] = pair_tile(state, "soft_gap", PAIRS + t // 2)
+                m_new[t // 2] = pair_tile(results, "m_new", t // 2)
+            nc.vector.scalar_tensor_tensor(out=gap[t // 2][:, t % 2, :], in0=wave[:], scalar=column(bias[:, INPUT, :], t), in1=log_fm[t // 2][:, t % 2, :], op0=ALU.add, op1=ALU.subtract)
+            nc.vector.scalar_tensor_tensor(out=m_new[t // 2][:, t % 2, :], in0=wave[:], scalar=column(bias[:, INPUT, :], t), in1=log_fm[t // 2][:, t % 2, :], op0=ALU.add, op1=ALU.max)
+            if t % 2 == 1:
+                nc.sync.dma_start(out=m_out[:, t - 1 : t + 1, :], in_=m_new[t // 2][:])
+
+        def s_cell(t):
+            if t % 2 == 0:
+                z_part[t // 2] = pair_tile(temps, "z_part", t // 2)
+            nc.scalar.activation(out=z_part[t // 2][:, t % 2, :], in_=wave_of[CELL * TILES + t][:], func=ACT.Tanh, bias=column(bias[:, CELL, :], t), scale=1.0)
+
+        def s_output(t):
+            o_part[t] = results.tile([P, BATCH], F32, tag="h_new", name="o_part%d" % t, bufs=4)
+            nc.scalar.activation(out=o_part[t][:], in_=wave_of[OUTPUT * TILES + t][:], func=ACT.Tanh, bias=column(half_bias_o, t), scale=0.5)
+
+        def v_h_new(t):
+            nc.vector.scalar_tensor_tensor(out=o_part[t][:], in0=o_part[t][:], scalar=1.0, in1=h_wave[t // 2][:, t % 2, :], op0=ALU.add, op1=ALU.mult)
+            nc.sync.dma_start(out=h_out[:, t, :], in_=o_part[t][:])
+
+        def rows(j):
+            return slice(2 * j, 2 * j + 2)
+
+        def v_m_plus_b(j):
+            m_plus_b[j] = pair_tile(temps, "m_plus_b", j)
+            for t in (2 * j, 2 * j + 1):
+                nc.vector.tensor_scalar(out=m_plus_b[j][:, t % 2, :], in0=m_old[:, t, :], scalar1=column(bias[:, FORGET, :], t), scalar2=None, op0=ALU.add)
+
+        def s_decay(j):
+            nc.scalar.activation(out=soft[j][:], in_=soft[j][:], func=ACT.Exp, scale=-1.0)
+
+        def s_logs(j):
+            nc.scalar.activation(out=soft[j][:], in_=soft[j][:], func=ACT.Ln, bias=one[:], scale=1.0)
+            log_n1[j] = pair_tile(state, "log_n1_old", j)
+            nc.scalar.activation(out=log_n1[j][:], in_=n_old[:, rows(j), :], func=ACT.Ln, bias=one[:], scale=1.0)
+
+        def v_log_fm(j):
+            nc.vector.tensor_tensor(out=log_fm[j][:], in0=log_fm[j][:], in1=soft[j][:], op=ALU.subtract)
+
+        def v_span(j):
+            span[j] = pair_tile(state, "span", j)
+            nc.vector.scalar_tensor_tensor(out=span[j][:], in0=gap[j][:], scalar=0.0, in1=log_n1[j][:], op0=ALU.max, op1=ALU.subtract)
+
+        def s_ratios(j):
+            shrink[j] = pair_tile(temps, "shrink", j)
+            nc.scalar.activation(out=shrink[j][:], in_=gap[j][:], func=ACT.Exp, scale=-1.0)
+            nc.scalar.activation(out=gap[j][:], in_=gap[j][:], func=ACT.Exp, scale=1.0)
+
+        def v_old_part(j):
+            old_part[j] = pair_tile(state, "log_n1_old", PAIRS + j)
+            nc.vector.scalar_tensor_tensor(out=old_part[j][:], in0=shrink[j][:], scalar=1.0, in1=c_old[:, rows(j), :], op0=ALU.min, op1=ALU.mult)
+
+        def v_new_part(j):
+            nc.vector.scalar_tensor_tensor(out=z_part[j][:], in0=gap[j][:], scalar=1.0, in1=z_part[j][:], op0=ALU.min, op1=ALU.mult)
+
+        def v_c_new(j):
+            nc.vector.tensor_tensor(out=old_part[j][:], in0=old_part[j][:], in1=z_part[j][:], op=ALU.add)
+            nc.sync.dma_start(out=c_out[:, rows(j), :], in_=old_part[j][:])
+
+        def s_norm(j):
+            n_new = pair_tile(results, "n_new", j)
+            nc.scalar.activation(out=n_new[:], in_=span[j][:], func=ACT.Exp, scale=-1.0)
+            nc.sync.dma_start(out=n_out[:, rows(j), :], in_=n_new[:])
+            nc.scalar.activation(out=span[j][:], in_=span[j][:], func=ACT.Exp, scale=1.0)
+
+        def v_h_wave(j):
+            h_wave[j] = pair_tile(state, "log_fm_h", PAIRS + j)
+            nc.vector.tensor_tensor(out=h_wave[j][:], in0=old_part[j][:], in1=span[j][:], op=ALU.mult)
+
+        def s_squash(j):
+            nc.scalar.activation(out=h_wave[j][:], in_=h_wave[j][:], func=ACT.Tanh, scale=1.0)
+
+        def v_halve(j):
+            nc.vector.tensor_scalar(out=h_wave[j][:], in0=h_wave[j][:], scalar1=0.5, scalar2=None, op0=ALU.mult)
+
+        def at(step, t):
+            if 0 <= t < TILES:
+                step(t)
+
+        def at_pair(step, t):
+            if 0 <= t < TILES and t % 2 == 1:
+                step(t // 2)
+
+        first_load = (RAW_AHEAD - 4) // 2
+        for s in range(-3, UNITS + 3):
+            if s % 2 == 0 and first_load <= (s + 2 + 2 * first_load) // 2 < UNITS // 2:
+                load_pair((s + 2 + 2 * first_load) // 2)
             if 0 <= s < UNITS:
                 multiply(s)
             if 0 <= s + 3 < UNITS:
                 turn(s + 3)
-
-            t = s - AT_FORGET
-            if in_tiles(t):
-                soft[t] = state.tile([P, BATCH], F32, tag="soft_gap", name="soft%d" % t)
-                nc.scalar.activation(out=soft[t][:], in_=wave_of[t][:], func=ACT.Abs, bias=column(bias[:, FORGET, :], t), scale=1.0)
-            nxt = s + 1
-            if 0 <= s + 2 < UNITS:
-                evacuate(s + 2, 0, nc.scalar.copy)
-                if (s + 2) // TILES in (FORGET, OUTPUT):
-                    evacuate(s + 2, 1, nc.vector.tensor_copy)
-                else:
-                    evacuate(s + 2, 1, nc.scalar.copy)
-            if in_tiles(t):
-                nc.scalar.activation(out=soft[t][:], in_=soft[t][:], func=ACT.Exp, scale=-1.0)
-                log_fm[t] = state.tile([P, BATCH], F32, tag="log_fm_h", name="log_fm%d" % t)
-                nc.vector.scalar_tensor_tensor(
-                    out=log_fm[t][:], in0=wave_of[t][:], scalar=column(minus_bias_f, t), in1=m_plus_b[t][:], op0=ALU.min, op1=ALU.add
-                )
-            t = s - AT_INPUT
-            if in_tiles(t):
-                nc.vector.tensor_tensor(out=log_fm[t][:], in0=log_fm[t][:], in1=soft[t][:], op=ALU.subtract)
-            if 0 <= nxt < UNITS:
-                quantise(nxt)
-            if in_tiles(t):
-                wave = wave_of[INPUT * TILES + t]
-                gap[t] = state.tile([P, BATCH], F32, tag="soft_gap", name="gap%d" % t)
-                nc.vector.scalar_tensor_tensor(
-                    out=gap[t][:], in0=wave[:], scalar=column(bias[:, INPUT, :], t), in1=log_fm[t][:], op0=ALU.add, op1=ALU.subtract
-                )
-                m_new = results.tile([P, BATCH], F32, tag="m_new", name="m_new%d" % t)
-                nc.vector.scalar_tensor_tensor(
-                    out=m_new[:], in0=wave[:], scalar=column(bias[:, INPUT, :], t), in1=log_fm[t][:], op0=ALU.add, op1=ALU.max
-                )
-                nc.sync.dma_start(out=m_out[:, t, :], in_=m_new[:])
-            t = s - AT_CELL
-            if in_tiles(t):
-                z_part[t] = temps.tile([P, BATCH], F32, tag="z_part", name="z_part%d" % t)
-                nc.scalar.activation(out=z_part[t][:], in_=wave_of[CELL * TILES + t][:], func=ACT.Tanh, bias=column(bias[:, CELL, :], t), scale=1.0)
-            t = s - AT_OUTPUT
-            if in_tiles(t):
-                o_part[t] = results.tile([P, BATCH], F32, tag="h_new", name="o_part%d" % t)
-                nc.scalar.activation(out=o_part[t][:], in_=wave_of[OUTPUT * TILES + t][:], func=ACT.Tanh, bias=column(half_bias_o, t), scale=0.5)
-            j = s - AT_LOGS
-            if 0 <= j < TILES // 2:
-                for t in (2 * j, 2 * j + 1):
-                    nc.scalar.activation(out=soft[t][:], in_=soft[t][:], func=ACT.Ln, bias=one[:], scale=1.0)
-                    log_n1[t] = state.tile([P, BATCH], F32, tag="log_n1", name="log_n1_%d" % t)
-                    nc.scalar.activation(out=log_n1[t][:], in_=n_old[:, t, :], func=ACT.Ln, bias=one[:], scale=1.0)
-            t = s - AT_SPAN
-            if in_tiles(t):
-                span[t] = state.tile([P, BATCH], F32, tag="span", name="span%d" % t)
-                nc.vector.scalar_tensor_tensor(out=span[t][:], in0=gap[t][:], scalar=0.0, in1=log_n1[t][:], op0=ALU.max, op1=ALU.subtract)
-            t = s - AT_CELL - 1
-            if in_tiles(t):
-                nc.vector.scalar_tensor_tensor(out=z_part[t][:], in0=gap[t][:], scalar=1.0, in1=z_part[t][:], op0=ALU.min, op1=ALU.mult)
-            t = s - AT_EXP - 1
-            if in_tiles(t):
-                old_part[t] = state.tile([P, BATCH], F32, tag="old_part", name="old_part%d" % t)
-                nc.vector.scalar_tensor_tensor(out=old_part[t][:], in0=shrink[t][:], scalar=1.0, in1=c_old[:, t, :], op0=ALU.min, op1=ALU.mult)
-            t = s - AT_CELL - 1
-            if in_tiles(t):
-                nc.vector.tensor_tensor(out=old_part[t][:], in0=old_part[t][:], in1=z_part[t][:], op=ALU.add)
-                nc.sync.dma_start(out=c_out[:, t, :], in_=old_part[t][:])
-            t = s - AT_NORM - 3
-            if in_tiles(t):
-                nc.vector.tensor_scalar(out=h_wave[t][:], in0=h_wave[t][:], scalar1=0.5, scalar2=None, op0=ALU.mult)
-            t = s - AT_NORM - 1
-            if in_tiles(t):
-                h_wave[t] = state.tile([P, BATCH], F32, tag="log_fm_h", name="h_wave%d" % t)
-                nc.vector.tensor_tensor(out=h_wave[t][:], in0=old_part[t][:], in1=span[t][:], op=ALU.mult)
-            t = s
-            if in_tiles(t):
-                m_plus_b[t] = temps.tile([P, BATCH], F32, tag="m_plus_b", name="m_plus_b%d" % t)
-                nc.vector.tensor_scalar(out=m_plus_b[t][:], in0=m_old[:, t, :], scalar1=column(bias[:, FORGET, :], t), scalar2=None, op0=ALU.add)
-            t = s - AT_OUTPUT
-            if in_tiles(t):
-                nc.vector.scalar_tensor_tensor(out=o_part[t][:], in0=o_part[t][:], scalar=1.0, in1=h_wave[t][:], op0=ALU.add, op1=ALU.mult)
-                nc.sync.dma_start(out=h_out[:, t, :], in_=o_part[t][:])
-            t = s - AT_EXP
-            if in_tiles(t):
-                shrink[t] = temps.tile([P, BATCH], F32, tag="shrink", name="shrink%d" % t)
-                nc.scalar.activation(out=shrink[t][:], in_=gap[t][:], func=ACT.Exp, scale=-1.0)
-                nc.scalar.activation(out=gap[t][:], in_=gap[t][:], func=ACT.Exp, scale=1.0)
-            t = s - AT_NORM
-            if in_tiles(t):
-                n_new = results.tile([P, BATCH], F32, tag="n_new", name="n_new%d" % t)
-                nc.scalar.activation(out=n_new[:], in_=span[t][:], func=ACT.Exp, scale=-1.0)
-                nc.sync.dma_start(out=n_out[:, t, :], in_=n_new[:])
-                nc.scalar.activation(out=span[t][:], in_=span[t][:], func=ACT.Exp, scale=1.0)
-            t = s - AT_NORM - 2
-            if in_tiles(t):
-                nc.scalar.activation(out=h_wave[t][:], in_=h_wave[t][:], func=ACT.Tanh, scale=1.0)
+            ev = s + 2
+            vector_takes_r = ev // (TILES // 2) in (0, 1, 2, 6, 7)
+            vector_takes_w = 0 <= s - AT_LOGS < 2
+            at(s_magnitude, s - AT_FORGET)
+            if 0 <= ev < UNITS:
+                if not vector_takes_w:
+                    evacuate(ev, 0, nc.scalar.copy)
+                if not vector_takes_r:
+                    evacuate(ev, 1, nc.scalar.copy)
+            at_pair(s_decay, s - AT_FORGET)
+            at(s_cell, s - AT_CELL)
+            at(s_output, s - AT_OUTPUT)
+            if 0 <= s - AT_LOGS < PAIRS:
+                s_logs(s - AT_LOGS)
+            at_pair(s_ratios, s - AT_EXP)
+            at_pair(s_norm, s - AT_NORM)
+            at_pair(s_squash, s - AT_NORM - 2)
+            at(v_h_new, s - AT_OUTPUT - 1)
+            if 0 <= s + 1 < UNITS:
+                quantise(s + 1)
+            at_pair(v_span, s - AT_SPAN)
+            at_pair(v_new_part, s - AT_CELL - 1)
+            at_pair(v_old_part, s - AT_EXP - 1)
+            at_pair(v_c_new, s - AT_CELL - 1)
+            at_pair(v_halve, s - AT_NORM - 3)
+            at_pair(v_h_wave, s - AT_NORM - 1)
+            at_pair(v_m_plus_b, s + 2)
+            if 0 <= s - AT_LOGS - 1 < PAIRS:
+                v_log_fm(s - AT_LOGS - 1)
+            if 0 <= ev < UNITS:
+                if vector_takes_w:
+                    evacuate(ev, 0, nc.vector.tensor_copy)
+                if vector_takes_r:
+                    evacuate(ev, 1, nc.vector.tensor_copy)
+            at(v_floor, s - AT_FORGET)
+            at(v_input, s - AT_INPUT)

@@ -15,23 +15,25 @@ P = 128
 FEATURES = 1024
 BATCH = 512
 TILES = FEATURES // P
+PAIRS = TILES // 2
 PACK = 4
-K_PASS = P * PACK
-PASSES = FEATURES // K_PASS
-GATES = 4
-UNITS = GATES * TILES
-FORGET, INPUT, CELL, OUTPUT = range(GATES)
+PASSES = FEATURES // (P * PACK)
 WORDS = FEATURES // 2
+GATES = 4
+FORGET, INPUT, CELL, OUTPUT = range(GATES)
+UNITS = GATES * TILES
+
 FLOPS = 2 * 2 * GATES * FEATURES * FEATURES * BATCH
 
 AT_FORGET = FORGET * TILES + 1
-AT_LOGS = AT_FORGET + TILES - 1
 AT_INPUT = INPUT * TILES + 1
 AT_CELL = CELL * TILES + 1
 AT_OUTPUT = OUTPUT * TILES + 1
-AT_EXP = AT_INPUT + 3
+AT_LOGS = AT_FORGET + TILES - 1
 AT_SPAN = AT_INPUT + 1
+AT_EXP = AT_LOGS + PAIRS
 AT_NORM = AT_OUTPUT - 4
+
 RAW_AHEAD = 10
 VECTOR_COLUMNS = 336
 
@@ -58,7 +60,7 @@ def tile_slstmcell_pa_kernel(
         raw_pool = ctx.enter_context(tc.tile_pool(name="raw", bufs=RAW_AHEAD))
         grouped_pool = ctx.enter_context(tc.tile_pool(name="grouped", bufs=3))
         codes_pool = ctx.enter_context(tc.tile_pool(name="codes", bufs=3))
-        state = ctx.enter_context(tc.tile_pool(name="state", bufs=TILES // 2))
+        state = ctx.enter_context(tc.tile_pool(name="state", bufs=PAIRS))
         temps = ctx.enter_context(tc.tile_pool(name="temps", bufs=2))
         results = ctx.enter_context(tc.tile_pool(name="results", bufs=2))
         turned_pool = ctx.enter_context(tc.psum_pool(name="turned", bufs=4))
@@ -78,10 +80,10 @@ def tile_slstmcell_pa_kernel(
 
         moving_raw = []
         for source in (x, h_prev):
-            halves = source.rearrange("(g u q e) b -> q g u (e b)", g=PASSES, u=2, e=2)
+            quarters = source.rearrange("(g u q e) b -> q g u (e b)", g=PASSES, u=2, e=2)
             for g in range(PASSES):
                 raw = raw_pool.tile([P, PACK, BATCH], BF16, tag="raw", name="moving_raw%d" % len(moving_raw))
-                nc.sync.dma_start(out=raw[:].rearrange("q (u e) b -> q u (e b)", e=2), in_=halves[:, g])
+                nc.sync.dma_start(out=raw[:].rearrange("q (u e) b -> q u (e b)", e=2), in_=quarters[:, g])
                 moving_raw.append(raw)
 
         raw_of = {}
@@ -94,25 +96,31 @@ def tile_slstmcell_pa_kernel(
                 raw_of[(pair, m)] = raw
             if gate == FORGET:
                 nc.sync.dma_start(out=m_old[:, first : first + 2, :], in_=by_tile(m_prev)[:, first : first + 2, :])
-            if pair == TILES // 2 - 1:
+            if pair == PAIRS - 1:
                 nc.sync.dma_start(out=n_old[:], in_=by_tile(n_prev))
-            if pair == TILES // 2 + 1:
+            if pair == PAIRS + 1:
                 nc.sync.dma_start(out=c_old[:], in_=by_tile(c_prev))
 
-        for pair in range((RAW_AHEAD - 4) // 2):
+        pairs_at_once = (RAW_AHEAD - len(moving_raw)) // 2
+        for pair in range(pairs_at_once):
             load_pair(pair)
 
-        for j in range(2 * PASSES):
-            grouped = grouped_pool.tile([P, BATCH, PACK], BF16, tag="grouped", name="moving_grouped%d" % j, align_bytes=64)
-            for engine_copy, cols in ((nc.vector.tensor_copy, slice(0, VECTOR_COLUMNS)), (nc.scalar.copy, slice(VECTOR_COLUMNS, BATCH))):
-                engine_copy(
-                    out=grouped[:, cols, :].rearrange("p (c i) t -> p c t i", i=4),
-                    in_=moving_raw[j][:, :, cols].rearrange("p t (c i) -> p c t i", i=4),
-                )
+        moving_grouped = []
+        for j in range(2 * PASSES + 1):
+            if j < 2 * PASSES:
+                grouped = grouped_pool.tile([P, BATCH, PACK], BF16, tag="grouped", name="moving_grouped%d" % j, align_bytes=64)
+                moving_grouped.append(grouped)
+                for engine_copy, cols in ((nc.vector.tensor_copy, slice(0, VECTOR_COLUMNS)), (nc.scalar.copy, slice(VECTOR_COLUMNS, BATCH))):
+                    engine_copy(
+                        out=grouped[:, cols, :].rearrange("p (c i) t -> p c t i", i=4),
+                        in_=moving_raw[j][:, :, cols].rearrange("p t (c i) -> p c t i", i=4),
+                    )
             if j > 0:
-                nc.vector.quantize_mx(out=moving_codes[:, j - 1, :].bitcast(FP8X4), scales=moving_scales[:, j - 1, :], in_=previous[:].rearrange("p b t -> p (b t)"))
-            previous = grouped
-        nc.vector.quantize_mx(out=moving_codes[:, 3, :].bitcast(FP8X4), scales=moving_scales[:, 3, :], in_=previous[:].rearrange("p b t -> p (b t)"))
+                nc.vector.quantize_mx(
+                    out=moving_codes[:, j - 1, :].bitcast(FP8X4),
+                    scales=moving_scales[:, j - 1, :],
+                    in_=moving_grouped[j - 1][:].rearrange("p b t -> p (b t)"),
+                )
 
         one = consts.tile([P, 1], F32, name="one")
         nc.vector.memset(one[:], 1.0)
@@ -122,6 +130,9 @@ def tile_slstmcell_pa_kernel(
         nc.vector.tensor_scalar(out=minus_bias_f[:], in0=bias[:, FORGET, :], scalar1=-1.0, scalar2=None, op0=ALU.mult)
         half_bias_o = consts.tile([P, TILES], F32, name="half_bias_o")
         nc.vector.tensor_scalar(out=half_bias_o[:], in0=bias[:, OUTPUT, :], scalar1=0.5, scalar2=None, op0=ALU.mult)
+
+        def column(table, t):
+            return table[:, t : t + 1]
 
         banks_of, grouped_of, codes_of, scales_of, wave_of = {}, {}, {}, {}, {}
 
@@ -136,9 +147,9 @@ def tile_slstmcell_pa_kernel(
         def evacuate(u, m, engine_copy):
             if u not in grouped_of:
                 grouped_of[u] = grouped_pool.tile([P, 2 * FEATURES], BF16, tag="grouped", name="grouped%d" % u, align_bytes=64)
-            pairs = grouped_of[u][:].bitcast(F32)[:, m * WORDS : (m + 1) * WORDS]
+            words = grouped_of[u][:].bitcast(F32)[:, m * WORDS : (m + 1) * WORDS]
             engine_copy(
-                out=pairs.rearrange("p (g h u) -> p g h u", g=PASSES, u=2),
+                out=words.rearrange("p (g h u) -> p g h u", g=PASSES, u=2),
                 in_=banks_of[(u, m)][:].rearrange("p (g u) h -> p g h u", u=2),
             )
 
@@ -152,19 +163,22 @@ def tile_slstmcell_pa_kernel(
             for j in range(2 * PASSES):
                 cols = slice(j * P, (j + 1) * P)
                 nc.tensor.matmul_mx(
-                    out=wave_of[u][:], lhsT=codes_of[u][:, cols].bitcast(FP8X4), lhsT_scale=scales_of[u][:, cols],
-                    rhs=moving_codes[:, j, :].bitcast(FP8X4), rhs_scale=moving_scales[:, j, :],
-                    start=(j == 0), stop=(j == 2 * PASSES - 1),
+                    out=wave_of[u][:],
+                    lhsT=codes_of[u][:, cols].bitcast(FP8X4),
+                    lhsT_scale=scales_of[u][:, cols],
+                    rhs=moving_codes[:, j, :].bitcast(FP8X4),
+                    rhs_scale=moving_scales[:, j, :],
+                    start=(j == 0),
+                    stop=(j == 2 * PASSES - 1),
                 )
 
-        m_plus_b, soft, log_fm, log_n1, gap, span, old_part, shrink, z_part, h_wave, o_part, m_new = ({} for k in range(12))
-        PAIRS = TILES // 2
-
-        def column(table, t):
-            return table[:, t : t + 1]
+        m_plus_b, soft, log_fm, log_n1, gap, span, c_new, shrink, z_part, h_wave, h_new, m_new = ({} for k in range(12))
 
         def pair_tile(pool, tag, j):
             return pool.tile([P, 2, BATCH], F32, tag=tag, name="%s%d" % (tag, j))
+
+        def rows(j):
+            return slice(2 * j, 2 * j + 2)
 
         def s_magnitude(t):
             if t % 2 == 0:
@@ -174,17 +188,23 @@ def tile_slstmcell_pa_kernel(
         def v_floor(t):
             if t % 2 == 0:
                 log_fm[t // 2] = pair_tile(state, "log_fm_h", t // 2)
-            nc.vector.scalar_tensor_tensor(out=log_fm[t // 2][:, t % 2, :], in0=wave_of[t][:], scalar=column(minus_bias_f, t), in1=m_plus_b[t // 2][:, t % 2, :], op0=ALU.min, op1=ALU.add)
+            nc.vector.scalar_tensor_tensor(
+                out=log_fm[t // 2][:, t % 2, :], in0=wave_of[t][:], scalar=column(minus_bias_f, t), in1=m_plus_b[t // 2][:, t % 2, :],
+                op0=ALU.min, op1=ALU.add,
+            )
 
         def v_input(t):
             wave = wave_of[INPUT * TILES + t]
             if t % 2 == 0:
                 gap[t // 2] = pair_tile(state, "soft_gap", PAIRS + t // 2)
                 m_new[t // 2] = pair_tile(results, "m_new", t // 2)
-            nc.vector.scalar_tensor_tensor(out=gap[t // 2][:, t % 2, :], in0=wave[:], scalar=column(bias[:, INPUT, :], t), in1=log_fm[t // 2][:, t % 2, :], op0=ALU.add, op1=ALU.subtract)
-            nc.vector.scalar_tensor_tensor(out=m_new[t // 2][:, t % 2, :], in0=wave[:], scalar=column(bias[:, INPUT, :], t), in1=log_fm[t // 2][:, t % 2, :], op0=ALU.add, op1=ALU.max)
+            for out, op1 in ((gap[t // 2], ALU.subtract), (m_new[t // 2], ALU.max)):
+                nc.vector.scalar_tensor_tensor(
+                    out=out[:, t % 2, :], in0=wave[:], scalar=column(bias[:, INPUT, :], t), in1=log_fm[t // 2][:, t % 2, :],
+                    op0=ALU.add, op1=op1,
+                )
             if t % 2 == 1:
-                nc.sync.dma_start(out=m_out[:, t - 1 : t + 1, :], in_=m_new[t // 2][:])
+                nc.sync.dma_start(out=m_out[:, rows(t // 2), :], in_=m_new[t // 2][:])
 
         def s_cell(t):
             if t % 2 == 0:
@@ -192,15 +212,12 @@ def tile_slstmcell_pa_kernel(
             nc.scalar.activation(out=z_part[t // 2][:, t % 2, :], in_=wave_of[CELL * TILES + t][:], func=ACT.Tanh, bias=column(bias[:, CELL, :], t), scale=1.0)
 
         def s_output(t):
-            o_part[t] = results.tile([P, BATCH], F32, tag="h_new", name="o_part%d" % t, bufs=4)
-            nc.scalar.activation(out=o_part[t][:], in_=wave_of[OUTPUT * TILES + t][:], func=ACT.Tanh, bias=column(half_bias_o, t), scale=0.5)
+            h_new[t] = results.tile([P, BATCH], F32, tag="h_new", name="h_new%d" % t, bufs=4)
+            nc.scalar.activation(out=h_new[t][:], in_=wave_of[OUTPUT * TILES + t][:], func=ACT.Tanh, bias=column(half_bias_o, t), scale=0.5)
 
         def v_h_new(t):
-            nc.vector.scalar_tensor_tensor(out=o_part[t][:], in0=o_part[t][:], scalar=1.0, in1=h_wave[t // 2][:, t % 2, :], op0=ALU.add, op1=ALU.mult)
-            nc.sync.dma_start(out=h_out[:, t, :], in_=o_part[t][:])
-
-        def rows(j):
-            return slice(2 * j, 2 * j + 2)
+            nc.vector.scalar_tensor_tensor(out=h_new[t][:], in0=h_new[t][:], scalar=1.0, in1=h_wave[t // 2][:, t % 2, :], op0=ALU.add, op1=ALU.mult)
+            nc.sync.dma_start(out=h_out[:, t, :], in_=h_new[t][:])
 
         def v_m_plus_b(j):
             m_plus_b[j] = pair_tile(temps, "m_plus_b", j)
@@ -212,7 +229,7 @@ def tile_slstmcell_pa_kernel(
 
         def s_logs(j):
             nc.scalar.activation(out=soft[j][:], in_=soft[j][:], func=ACT.Ln, bias=one[:], scale=1.0)
-            log_n1[j] = pair_tile(state, "log_n1_old", j)
+            log_n1[j] = pair_tile(state, "log_n1_c", j)
             nc.scalar.activation(out=log_n1[j][:], in_=n_old[:, rows(j), :], func=ACT.Ln, bias=one[:], scale=1.0)
 
         def v_log_fm(j):
@@ -228,15 +245,15 @@ def tile_slstmcell_pa_kernel(
             nc.scalar.activation(out=gap[j][:], in_=gap[j][:], func=ACT.Exp, scale=1.0)
 
         def v_old_part(j):
-            old_part[j] = pair_tile(state, "log_n1_old", PAIRS + j)
-            nc.vector.scalar_tensor_tensor(out=old_part[j][:], in0=shrink[j][:], scalar=1.0, in1=c_old[:, rows(j), :], op0=ALU.min, op1=ALU.mult)
+            c_new[j] = pair_tile(state, "log_n1_c", PAIRS + j)
+            nc.vector.scalar_tensor_tensor(out=c_new[j][:], in0=shrink[j][:], scalar=1.0, in1=c_old[:, rows(j), :], op0=ALU.min, op1=ALU.mult)
 
         def v_new_part(j):
             nc.vector.scalar_tensor_tensor(out=z_part[j][:], in0=gap[j][:], scalar=1.0, in1=z_part[j][:], op0=ALU.min, op1=ALU.mult)
 
         def v_c_new(j):
-            nc.vector.tensor_tensor(out=old_part[j][:], in0=old_part[j][:], in1=z_part[j][:], op=ALU.add)
-            nc.sync.dma_start(out=c_out[:, rows(j), :], in_=old_part[j][:])
+            nc.vector.tensor_tensor(out=c_new[j][:], in0=c_new[j][:], in1=z_part[j][:], op=ALU.add)
+            nc.sync.dma_start(out=c_out[:, rows(j), :], in_=c_new[j][:])
 
         def s_norm(j):
             n_new = pair_tile(results, "n_new", j)
@@ -246,7 +263,7 @@ def tile_slstmcell_pa_kernel(
 
         def v_h_wave(j):
             h_wave[j] = pair_tile(state, "log_fm_h", PAIRS + j)
-            nc.vector.tensor_tensor(out=h_wave[j][:], in0=old_part[j][:], in1=span[j][:], op=ALU.mult)
+            nc.vector.tensor_tensor(out=h_wave[j][:], in0=c_new[j][:], in1=span[j][:], op=ALU.mult)
 
         def s_squash(j):
             nc.scalar.activation(out=h_wave[j][:], in_=h_wave[j][:], func=ACT.Tanh, scale=1.0)
@@ -262,47 +279,52 @@ def tile_slstmcell_pa_kernel(
             if 0 <= t < TILES and t % 2 == 1:
                 step(t // 2)
 
-        first_load = (RAW_AHEAD - 4) // 2
-        for s in range(-3, UNITS + 3):
-            if s % 2 == 0 and first_load <= (s + 2 + 2 * first_load) // 2 < UNITS // 2:
-                load_pair((s + 2 + 2 * first_load) // 2)
+        def at_each_pair(step, j):
+            if 0 <= j < PAIRS:
+                step(j)
+
+        for s in range(-3, UNITS + 2):
+            if s % 2 == 0 and pairs_at_once <= s // 2 + pairs_at_once + 1 < UNITS // 2:
+                load_pair(s // 2 + pairs_at_once + 1)
+
             if 0 <= s < UNITS:
                 multiply(s)
             if 0 <= s + 3 < UNITS:
                 turn(s + 3)
-            ev = s + 2
-            vector_takes_r = ev // (TILES // 2) in (0, 1, 2, 6, 7)
-            vector_takes_w = 0 <= s - AT_LOGS < 2
+
+            emptied = s + 2
+            gate, tile_in_gate = divmod(emptied, TILES)
+            vector_takes = []
+            if 0 <= s - AT_LOGS < PAIRS - 1:
+                vector_takes.append(0)
+            if gate in (FORGET, OUTPUT) or (gate == INPUT and tile_in_gate < PAIRS):
+                vector_takes.append(1)
+
             at(s_magnitude, s - AT_FORGET)
-            if 0 <= ev < UNITS:
-                if not vector_takes_w:
-                    evacuate(ev, 0, nc.scalar.copy)
-                if not vector_takes_r:
-                    evacuate(ev, 1, nc.scalar.copy)
+            for m in range(2):
+                if 0 <= emptied < UNITS and m not in vector_takes:
+                    evacuate(emptied, m, nc.scalar.copy)
             at_pair(s_decay, s - AT_FORGET)
             at(s_cell, s - AT_CELL)
             at(s_output, s - AT_OUTPUT)
-            if 0 <= s - AT_LOGS < PAIRS:
-                s_logs(s - AT_LOGS)
+            at_each_pair(s_logs, s - AT_LOGS)
             at_pair(s_ratios, s - AT_EXP)
             at_pair(s_norm, s - AT_NORM)
             at_pair(s_squash, s - AT_NORM - 2)
+
             at(v_h_new, s - AT_OUTPUT - 1)
+            at_pair(v_new_part, s - AT_CELL - 1)
             if 0 <= s + 1 < UNITS:
                 quantise(s + 1)
             at_pair(v_span, s - AT_SPAN)
-            at_pair(v_new_part, s - AT_CELL - 1)
             at_pair(v_old_part, s - AT_EXP - 1)
             at_pair(v_c_new, s - AT_CELL - 1)
             at_pair(v_halve, s - AT_NORM - 3)
             at_pair(v_h_wave, s - AT_NORM - 1)
             at_pair(v_m_plus_b, s + 2)
-            if 0 <= s - AT_LOGS - 1 < PAIRS:
-                v_log_fm(s - AT_LOGS - 1)
-            if 0 <= ev < UNITS:
-                if vector_takes_w:
-                    evacuate(ev, 0, nc.vector.tensor_copy)
-                if vector_takes_r:
-                    evacuate(ev, 1, nc.vector.tensor_copy)
+            for m in range(2):
+                if 0 <= emptied < UNITS and m in vector_takes:
+                    evacuate(emptied, m, nc.vector.tensor_copy)
             at(v_floor, s - AT_FORGET)
+            at_each_pair(v_log_fm, s - AT_LOGS - 1)
             at(v_input, s - AT_INPUT)

from contextlib import ExitStack

import concourse.mybir as mybir
from concourse.masks import make_identity

F32 = mybir.dt.float32
BF16 = mybir.dt.bfloat16
U32 = mybir.dt.uint32
U8 = mybir.dt.uint8
FP8X4 = mybir.dt.float8_e4m3fn_x4
ACT = mybir.ActivationFunctionType
ALU = mybir.AluOpType

P = 128
FEATURES = 1024
BATCH = 512
TILES = FEATURES // P
PAIRS = TILES // 2
PACK = 4
PASSES = FEATURES // (P * PACK)
WORDS = FEATURES // 2
GATES = 4
FORGET, INPUT, CELL, OUTPUT = range(GATES)
UNITS = GATES * TILES

FLOPS = 2 * 2 * GATES * FEATURES * FEATURES * BATCH

AT_FORGET = FORGET * TILES + 1
AT_INPUT = INPUT * TILES + 1
AT_CELL = CELL * TILES + 1
AT_OUTPUT = OUTPUT * TILES + 1
AT_LOGS = AT_FORGET + TILES - 1
AT_SPAN = AT_INPUT + 1
AT_EXP = AT_LOGS + PAIRS
AT_NORM = AT_OUTPUT - 4

RAW_AHEAD = 10
VECTOR_COLUMNS = 336


def tile_slstmcell_pa_kernel(
    tc, x, h_prev, c_prev, n_prev, m_prev,
    w_input, w_forget, w_output, w_z, r_input, r_forget, r_output, r_z,
    b_input, b_forget, b_output, b_z,
    out_0, out_1, out_2, out_3,
):
    nc = tc.nc
    w_of = (w_forget, w_input, w_z, w_output)
    r_of = (r_forget, r_input, r_z, r_output)
    b_of = (b_forget, b_input, b_z, b_output)

    def by_tile(a):
        return a.rearrange("(p t) c -> p t c", t=TILES)

    h_out, c_out, n_out, m_out = by_tile(out_0), by_tile(out_1), by_tile(out_2), by_tile(out_3)

    with ExitStack() as ctx:
        ctx.enter_context(tc.manual_schedule())
        consts = ctx.enter_context(tc.tile_pool(name="consts", bufs=1))
        raw_pool = ctx.enter_context(tc.tile_pool(name="raw", bufs=RAW_AHEAD))
        grouped_pool = ctx.enter_context(tc.tile_pool(name="grouped", bufs=3))
        codes_pool = ctx.enter_context(tc.tile_pool(name="codes", bufs=3))
        state = ctx.enter_context(tc.tile_pool(name="state", bufs=PAIRS))
        temps = ctx.enter_context(tc.tile_pool(name="temps", bufs=2))
        results = ctx.enter_context(tc.tile_pool(name="results", bufs=2))
        turned_pool = ctx.enter_context(tc.psum_pool(name="turned", bufs=4))
        wave_pool = ctx.enter_context(tc.psum_pool(name="waves", bufs=4))

        identity = consts.tile([P, P], F32, name="identity")
        make_identity(nc, identity[:])
        bias_bf = consts.tile([P, GATES, 2 * TILES], BF16, name="bias_bf")
        for gate in range(GATES):
            nc.scalar.dma_start(out=bias_bf[:, gate, 0:TILES], in_=b_of[gate].rearrange("(p t) -> p t", t=TILES))

        moving_codes = consts.tile([P, 2 * PASSES, BATCH], U32, name="moving_codes", align_bytes=64)
        moving_scales = consts.tile([P, 2 * PASSES, BATCH], U8, name="moving_scales", align_bytes=64)
        m_old = consts.tile([P, TILES, BATCH], BF16, name="m_old")
        n_old = consts.tile([P, TILES, BATCH], BF16, name="n_old")
        c_old = consts.tile([P, TILES, BATCH], BF16, name="c_old")

        moving_raw = []
        for source in (x, h_prev):
            quarters = source.rearrange("(g u q e) b -> q g u (e b)", g=PASSES, u=2, e=2)
            for g in range(PASSES):
                raw = raw_pool.tile([P, PACK, BATCH], BF16, tag="raw", name="moving_raw%d" % len(moving_raw))
                nc.sync.dma_start(out=raw[:].rearrange("q (u e) b -> q u (e b)", e=2), in_=quarters[:, g])
                moving_raw.append(raw)

        raw_of = {}

        def load_pair(pair):
            gate, first = divmod(2 * pair, TILES)
            for m, matrix in enumerate((w_of[gate], r_of[gate])):
                raw = raw_pool.tile([P, 2, FEATURES], BF16, tag="raw", name="raw%d_%d" % (pair, m))
                nc.sync.dma_start(out=raw[:], in_=by_tile(matrix)[:, first : first + 2, :])
                raw_of[(pair, m)] = raw
            if gate == FORGET:
                nc.sync.dma_start(out=m_old[:, first : first + 2, :], in_=by_tile(m_prev)[:, first : first + 2, :])
            if pair == PAIRS - 1:
                nc.sync.dma_start(out=n_old[:], in_=by_tile(n_prev))
            if pair == PAIRS + 1:
                nc.sync.dma_start(out=c_old[:], in_=by_tile(c_prev))

        pairs_at_once = (RAW_AHEAD - len(moving_raw)) // 2
        for pair in range(pairs_at_once):
            load_pair(pair)

        moving_grouped = []
        for j in range(2 * PASSES + 1):
            if j < 2 * PASSES:
                grouped = grouped_pool.tile([P, BATCH, PACK], BF16, tag="grouped", name="moving_grouped%d" % j, align_bytes=64)
                moving_grouped.append(grouped)
                for engine_copy, cols in ((nc.vector.tensor_copy, slice(0, VECTOR_COLUMNS)), (nc.scalar.copy, slice(VECTOR_COLUMNS, BATCH))):
                    engine_copy(
                        out=grouped[:, cols, :].rearrange("p (c i) t -> p c t i", i=4),
                        in_=moving_raw[j][:, :, cols].rearrange("p t (c i) -> p c t i", i=4),
                    )
            if j > 0:
                nc.vector.quantize_mx(
                    out=moving_codes[:, j - 1, :].bitcast(FP8X4),
                    scales=moving_scales[:, j - 1, :],
                    in_=moving_grouped[j - 1][:].rearrange("p b t -> p (b t)"),
                )

        one = consts.tile([P, 1], F32, name="one")
        nc.vector.memset(one[:], 1.0)
        bias = consts.tile([P, GATES, TILES], F32, name="bias")
        nc.vector.tensor_copy(out=bias[:], in_=bias_bf[:, :, 0:TILES])
        minus_bias_f = consts.tile([P, TILES], F32, name="minus_bias_f")
        nc.vector.tensor_scalar(out=minus_bias_f[:], in0=bias[:, FORGET, :], scalar1=-1.0, scalar2=None, op0=ALU.mult)
        half_bias_o = consts.tile([P, TILES], F32, name="half_bias_o")
        nc.vector.tensor_scalar(out=half_bias_o[:], in0=bias[:, OUTPUT, :], scalar1=0.5, scalar2=None, op0=ALU.mult)

        def column(table, t):
            return table[:, t : t + 1]

        banks_of, grouped_of, codes_of, scales_of, wave_of = {}, {}, {}, {}, {}

        def turn(u):
            for m in range(2):
                words = raw_of[(u // 2, m)][:, u % 2, :].bitcast(F32)
                bank = turned_pool.tile([P, 2 * PASSES, P], F32, tag="turned", name="turned%d_%d" % (u, m))
                for c in range(2 * PASSES):
                    nc.tensor.transpose(bank[:, c, :], words[:, c * P : (c + 1) * P], identity[:])
                banks_of[(u, m)] = bank

        def evacuate(u, m, engine_copy):
            if u not in grouped_of:
                grouped_of[u] = grouped_pool.tile([P, 2 * FEATURES], BF16, tag="grouped", name="grouped%d" % u, align_bytes=64)
            words = grouped_of[u][:].bitcast(F32)[:, m * WORDS : (m + 1) * WORDS]
            engine_copy(
                out=words.rearrange("p (g h u) -> p g h u", g=PASSES, u=2),
                in_=banks_of[(u, m)][:].rearrange("p (g u) h -> p g h u", u=2),
            )

        def quantise(u):
            codes_of[u] = codes_pool.tile([P, 2 * PASSES * P], U32, tag="codes", name="codes%d" % u, align_bytes=64)
            scales_of[u] = codes_pool.tile([P, 2 * PASSES * P], U8, tag="scales", name="scales%d" % u, align_bytes=64)
            nc.vector.quantize_mx(out=codes_of[u][:].bitcast(FP8X4), scales=scales_of[u][:], in_=grouped_of[u][:])

        def multiply(u):
            wave_of[u] = wave_pool.tile([P, BATCH], F32, tag="wave", name="wave%d" % u)
            for j in range(2 * PASSES):
                cols = slice(j * P, (j + 1) * P)
                nc.tensor.matmul_mx(
                    out=wave_of[u][:],
                    lhsT=codes_of[u][:, cols].bitcast(FP8X4),
                    lhsT_scale=scales_of[u][:, cols],
                    rhs=moving_codes[:, j, :].bitcast(FP8X4),
                    rhs_scale=moving_scales[:, j, :],
                    start=(j == 0),
                    stop=(j == 2 * PASSES - 1),
                )

        m_plus_b, soft, log_fm, log_n1, gap, span, c_new, shrink, z_part, h_wave, h_new, m_new = ({} for k in range(12))

        def pair_tile(pool, tag, j):
            return pool.tile([P, 2, BATCH], F32, tag=tag, name="%s%d" % (tag, j))

        def rows(j):
            return slice(2 * j, 2 * j + 2)

        def s_magnitude(t):
            if t % 2 == 0:
                soft[t // 2] = pair_tile(state, "soft_gap", t // 2)
            nc.scalar.activation(out=soft[t // 2][:, t % 2, :], in_=wave_of[t][:], func=ACT.Abs, bias=column(bias[:, FORGET, :], t), scale=1.0)

        def v_floor(t):
            if t % 2 == 0:
                log_fm[t // 2] = pair_tile(state, "log_fm_h", t // 2)
            nc.vector.scalar_tensor_tensor(
                out=log_fm[t // 2][:, t % 2, :], in0=wave_of[t][:], scalar=column(minus_bias_f, t), in1=m_plus_b[t // 2][:, t % 2, :],
                op0=ALU.min, op1=ALU.add,
            )

        def v_input(t):
            wave = wave_of[INPUT * TILES + t]
            if t % 2 == 0:
                gap[t // 2] = pair_tile(state, "soft_gap", PAIRS + t // 2)
                m_new[t // 2] = pair_tile(results, "m_new", t // 2)
            for out, op1 in ((gap[t // 2], ALU.subtract), (m_new[t // 2], ALU.max)):
                nc.vector.scalar_tensor_tensor(
                    out=out[:, t % 2, :], in0=wave[:], scalar=column(bias[:, INPUT, :], t), in1=log_fm[t // 2][:, t % 2, :],
                    op0=ALU.add, op1=op1,
                )
            if t % 2 == 1:
                nc.sync.dma_start(out=m_out[:, rows(t // 2), :], in_=m_new[t // 2][:])

        def s_cell(t):
            if t % 2 == 0:
                z_part[t // 2] = pair_tile(temps, "z_part", t // 2)
            nc.scalar.activation(out=z_part[t // 2][:, t % 2, :], in_=wave_of[CELL * TILES + t][:], func=ACT.Tanh, bias=column(bias[:, CELL, :], t), scale=1.0)

        def s_output(t):
            h_new[t] = results.tile([P, BATCH], F32, tag="h_new", name="h_new%d" % t, bufs=4)
            nc.scalar.activation(out=h_new[t][:], in_=wave_of[OUTPUT * TILES + t][:], func=ACT.Tanh, bias=column(half_bias_o, t), scale=0.5)

        def v_h_new(t):
            nc.vector.scalar_tensor_tensor(out=h_new[t][:], in0=h_new[t][:], scalar=1.0, in1=h_wave[t // 2][:, t % 2, :], op0=ALU.add, op1=ALU.mult)
            nc.sync.dma_start(out=h_out[:, t, :], in_=h_new[t][:])

        def v_m_plus_b(j):
            m_plus_b[j] = pair_tile(temps, "m_plus_b", j)
            for t in (2 * j, 2 * j + 1):
                nc.vector.tensor_scalar(out=m_plus_b[j][:, t % 2, :], in0=m_old[:, t, :], scalar1=column(bias[:, FORGET, :], t), scalar2=None, op0=ALU.add)

        def s_decay(j):
            nc.scalar.activation(out=soft[j][:], in_=soft[j][:], func=ACT.Exp, scale=-1.0)

        def s_logs(j):
            nc.scalar.activation(out=soft[j][:], in_=soft[j][:], func=ACT.Ln, bias=one[:], scale=1.0)
            log_n1[j] = pair_tile(state, "log_n1_c", j)
            nc.scalar.activation(out=log_n1[j][:], in_=n_old[:, rows(j), :], func=ACT.Ln, bias=one[:], scale=1.0)

        def v_log_fm(j):
            nc.vector.tensor_tensor(out=log_fm[j][:], in0=log_fm[j][:], in1=soft[j][:], op=ALU.subtract)

        def v_span(j):
            span[j] = pair_tile(state, "span", j)
            nc.vector.scalar_tensor_tensor(out=span[j][:], in0=gap[j][:], scalar=0.0, in1=log_n1[j][:], op0=ALU.max, op1=ALU.subtract)

        def s_ratios(j):
            shrink[j] = pair_tile(temps, "shrink", j)
            nc.scalar.activation(out=shrink[j][:], in_=gap[j][:], func=ACT.Exp, scale=-1.0)
            nc.scalar.activation(out=gap[j][:], in_=gap[j][:], func=ACT.Exp, scale=1.0)

        def v_old_part(j):
            c_new[j] = pair_tile(state, "log_n1_c", PAIRS + j)
            nc.vector.scalar_tensor_tensor(out=c_new[j][:], in0=shrink[j][:], scalar=1.0, in1=c_old[:, rows(j), :], op0=ALU.min, op1=ALU.mult)

        def v_new_part(j):
            nc.vector.scalar_tensor_tensor(out=z_part[j][:], in0=gap[j][:], scalar=1.0, in1=z_part[j][:], op0=ALU.min, op1=ALU.mult)

        def v_c_new(j):
            nc.vector.tensor_tensor(out=c_new[j][:], in0=c_new[j][:], in1=z_part[j][:], op=ALU.add)
            nc.sync.dma_start(out=c_out[:, rows(j), :], in_=c_new[j][:])

        def s_norm(j):
            n_new = pair_tile(results, "n_new", j)
            nc.scalar.activation(out=n_new[:], in_=span[j][:], func=ACT.Exp, scale=-1.0)
            nc.sync.dma_start(out=n_out[:, rows(j), :], in_=n_new[:])
            nc.scalar.activation(out=span[j][:], in_=span[j][:], func=ACT.Exp, scale=1.0)

        def v_h_wave(j):
            h_wave[j] = pair_tile(state, "log_fm_h", PAIRS + j)
            nc.vector.tensor_tensor(out=h_wave[j][:], in0=c_new[j][:], in1=span[j][:], op=ALU.mult)

        def s_squash(j):
            nc.scalar.activation(out=h_wave[j][:], in_=h_wave[j][:], func=ACT.Tanh, scale=1.0)

        def v_halve(j):
            nc.vector.tensor_scalar(out=h_wave[j][:], in0=h_wave[j][:], scalar1=0.5, scalar2=None, op0=ALU.mult)

        def at(step, t):
            if 0 <= t < TILES:
                step(t)

        def at_pair(step, t):
            if 0 <= t < TILES and t % 2 == 1:
                step(t // 2)

        def at_each_pair(step, j):
            if 0 <= j < PAIRS:
                step(j)

        for s in range(-3, UNITS + 2):
            if s % 2 == 0 and pairs_at_once <= s // 2 + pairs_at_once + 1 < UNITS // 2:
                load_pair(s // 2 + pairs_at_once + 1)

            if 0 <= s < UNITS:
                multiply(s)
            if 0 <= s + 3 < UNITS:
                turn(s + 3)

            emptied = s + 2
            gate, tile_in_gate = divmod(emptied, TILES)
            vector_takes = []
            if 0 <= s - AT_LOGS < PAIRS - 1:
                vector_takes.append(0)
            if gate in (FORGET, OUTPUT) or (gate == INPUT and tile_in_gate < PAIRS):
                vector_takes.append(1)

            at(s_magnitude, s - AT_FORGET)
            for m in range(2):
                if 0 <= emptied < UNITS and m not in vector_takes:
                    evacuate(emptied, m, nc.scalar.copy)
            at_pair(s_decay, s - AT_FORGET)
            at(s_cell, s - AT_CELL)
            at(s_output, s - AT_OUTPUT)
            at_each_pair(s_logs, s - AT_LOGS)
            at_pair(s_ratios, s - AT_EXP)
            at_pair(s_norm, s - AT_NORM)
            at_pair(s_squash, s - AT_NORM - 2)

            at(v_h_new, s - AT_OUTPUT - 1)
            at_pair(v_new_part, s - AT_CELL - 1)
            if 0 <= s + 1 < UNITS:
                quantise(s + 1)
            at_pair(v_span, s - AT_SPAN)
            at_pair(v_old_part, s - AT_EXP - 1)
            at_pair(v_c_new, s - AT_CELL - 1)
            at_pair(v_halve, s - AT_NORM - 3)
            at_pair(v_h_wave, s - AT_NORM - 1)
            at_pair(v_m_plus_b, s + 2)
            for m in range(2):
                if 0 <= emptied < UNITS and m in vector_takes:
                    evacuate(emptied, m, nc.vector.tensor_copy)
            at(v_floor, s - AT_FORGET)
            at_each_pair(v_log_fm, s - AT_LOGS - 1)
            at(v_input, s - AT_INPUT)
